import numpy as np
import ml_dtypes


def mxq(x, axis, fmt="e4m3"):
    dtype, down = {"e4m3": (ml_dtypes.float8_e4m3fn, 7), "e5m2": (ml_dtypes.float8_e5m2, 14)}[fmt]
    v = np.moveaxis(np.asarray(x, np.float32).astype(ml_dtypes.bfloat16).astype(np.float64), axis, -1)
    blocks = v.reshape(v.shape[:-1] + (-1, 32))
    amax = np.abs(blocks).max(-1, keepdims=True)
    byte = np.maximum(np.where(amax > 0, np.frexp(amax)[1] - 1 + 127, 0) - down, 1)
    scale = np.exp2(byte - 127.0)
    codes = (blocks / scale).astype(np.float32).astype(dtype).astype(np.float64)
    return np.moveaxis((codes * scale).reshape(v.shape), -1, axis)


WIDE = False


def mx_kscale(k):
    if not WIDE:
        return np.ones(k)
    levels = np.array([10, -10, 5, -5, 0])
    if k % 512:
        return np.exp2(np.random.permutation(np.resize(levels, k // 32))).repeat(32)
    a = np.empty((k // 512, 16))
    for p in range(k // 512):
        a[p, :8] = np.random.permutation(np.resize(levels, 8))
        for g in range(8):
            far = levels[np.abs(levels - a[p, g]) >= 10]
            a[p, g + 8] = far[np.random.randint(len(far))]
    return np.exp2(a.ravel()).repeat(32)


BF16 = ml_dtypes.bfloat16


def bf(x):
    return np.asarray(x, np.float32).astype(BF16)


def f64(x):
    return np.asarray(x).astype(np.float64)


B, N, IN_DIM, OUT_DIM, K = 8, 512, 512, 128, 3
EPS = 1e-6
SIG = 2.0


def laplacian(adj):
    d = adj.sum(axis=2)
    r = (d + EPS) ** -0.5
    return np.eye(N)[None] - r[:, :, None] * adj * r[:, None, :]


def setup_inputs():
    s, u = mx_kscale(N), mx_kscale(IN_DIM)
    sn = s / s.max()
    return {"x": bf(np.random.standard_normal((B, N, IN_DIM)) * sn[:, None] * u),
            "tx1": bf(np.random.standard_normal((B, N, IN_DIM)) * sn[:, None] * u),
            "adj": bf(np.exp(SIG * np.random.standard_normal((B, N, N)) - SIG * SIG / 2.0) / N * (s * s)[:, None]),
            "W": bf(np.random.standard_normal((K, IN_DIM, OUT_DIM)) / np.sqrt(IN_DIM) / u[:, None]),
            "b": bf(np.random.standard_normal((K, OUT_DIM)) * 0.3)}


def reference(x, tx1, adj, W, b):
    x, tx1, b = f64(x), f64(tx1), f64(b)
    Wq = mxq(f64(W), 1, "e4m3")
    L = laplacian(f64(adj))
    out = (mxq(x, 2, "e4m3") @ Wq[0]) + b[0] + (mxq(tx1, 2, "e4m3") @ Wq[1]) + b[1]
    tx2 = 2.0 * (mxq(L, 2, "e4m3") @ mxq(tx1, 1, "e4m3")) - x
    out = out + (mxq(tx2, 2, "e4m3") @ Wq[2]) + b[2]
    return np.maximum(out, 0.0)

@@ -1,0 +1,313 @@
+from contextlib import ExitStack
+
+import concourse.mybir as mybir
+from concourse.masks import make_identity
+
+F32 = mybir.dt.float32
+BF16 = mybir.dt.bfloat16
+U32 = mybir.dt.uint32
+U8 = mybir.dt.uint8
+FP8X4 = mybir.dt.float8_e4m3fn_x4
+ALU = mybir.AluOpType
+ACT = mybir.ActivationFunctionType
+
+P = 128
+PACK = 4
+GRAPHS = 8
+NODES = 512
+FEATS = 512
+OUTS = 128
+ORDERS = 3
+TILES = NODES // P
+EPS = 1e-6
+
+FLOPS = 2 * GRAPHS * (NODES * NODES * FEATS + ORDERS * NODES * FEATS * OUTS)
+
+
+def tile_cheblayer_pb_kernel(tc, x, tx1, adj, W, b, out):
+    nc = tc.nc
+    with ExitStack() as ctx:
+        const = ctx.enter_context(tc.tile_pool(name="const", bufs=1))
+        inputs = ctx.enter_context(tc.tile_pool(name="inputs", bufs=GRAPHS))
+        small = ctx.enter_context(tc.tile_pool(name="small", bufs=3))
+        work = ctx.enter_context(tc.tile_pool(name="work", bufs=2))
+        chain = ctx.enter_context(tc.psum_pool(name="chain", bufs=TILES))
+        turned = ctx.enter_context(tc.psum_pool(name="turned", bufs=4))
+        ctx.enter_context(tc.manual_schedule())
+
+        x_nat, tx1_nat, adj_nat = {}, {}, {}
+        deg, root, inv, rows = {}, {}, {}, {}
+        x_grp, lap_q, tx1_node_q, x_q, tx1_feat_q, tx2_q = {}, {}, {}, {}, {}, {}
+        tx1_feat_grp, tx1_node_grp, lap_grp, tx2_grp = {}, {}, {}, {}
+        rows_turned, prod, out_by_feat, out_turned, out_by_node = {}, {}, {}, {}, {}
+
+        eps = const.tile([P, 1], F32)
+        nc.vector.memset(eps[:], EPS)
+        warm = const.tile([P, 1], F32)
+        nc.scalar.activation(out=warm[:], in_=eps[:], func=ACT.Sqrt)
+        ident = const.tile([P, P], F32)
+        make_identity(nc, ident[:])
+        scrap = const.tile([P, TILES, NODES], BF16)
+
+        def load_adjacency(g, pieces):
+            adj_t = inputs.tile([P, TILES, NODES], BF16, tag="adj_nat")
+            adj_rows = adj[g].rearrange("(p a) j -> p a j", p=P)
+            step = TILES // pieces
+            for a in range(0, TILES, step):
+                nc.sync.dma_start(out=adj_t[:, a : a + step, :], in_=adj_rows[:, a : a + step, :])
+            adj_nat[g] = adj_t
+
+        def load_features(g):
+            tx1_t = inputs.tile([P, TILES, FEATS], BF16, tag="tx1_nat")
+            nc.sync.dma_start(out=tx1_t[:], in_=tx1[g].rearrange("(p a) f -> p a f", p=P))
+            x_t = inputs.tile([P, TILES, FEATS], BF16, tag="x_nat")
+            nc.sync.dma_start(out=x_t[:], in_=x[g].rearrange("(p a) f -> p a f", p=P))
+            tx1_nat[g], x_nat[g] = tx1_t, x_t
+
+        load_adjacency(0, pieces=TILES)
+        w_nat = const.tile([P, ORDERS, PACK * OUTS], BF16)
+        nc.sync.dma_start(out=w_nat[:], in_=W.rearrange("k (p t) o -> p k (t o)", t=PACK))
+        b_all = const.tile([P, ORDERS * OUTS], BF16)
+        nc.sync.dma_start(out=b_all[:], in_=b.rearrange("k o -> (k o)").partition_broadcast(P))
+        load_features(0)
+        for g in range(1, GRAPHS):
+            load_adjacency(g, pieces=1)
+            load_features(g)
+
+        def mx_operand(tag):
+            codes = work.tile([P, NODES], U32, tag=tag + "_codes", name=tag + "_codes", align_bytes=64)
+            scales = work.tile([P, NODES], U8, tag=tag + "_scales", name=tag + "_scales", align_bytes=64)
+            return codes, scales
+
+        def quantise_cols(grouped, operand, cols):
+            nc.vector.quantize_mx(
+                out=operand[0][:, cols].bitcast(FP8X4),
+                scales=operand[1][:, cols],
+                in_=grouped[:, cols, :].rearrange("p c t -> p (c t)"),
+            )
+
+        def quantise(grouped, tag):
+            operand = mx_operand(tag)
+            quantise_cols(grouped, operand, slice(0, NODES))
+            return operand
+
+        def mx(out_ap, stationary, s_cols, moving, m_cols, start, stop):
+            nc.tensor.matmul_mx(
+                out=out_ap,
+                lhsT=stationary[0][:, s_cols].bitcast(FP8X4),
+                lhsT_scale=stationary[1][:, s_cols],
+                rhs=moving[0][:, m_cols].bitcast(FP8X4),
+                rhs_scale=moving[1][:, m_cols],
+                start=start,
+                stop=stop,
+            )
+
+        def tile_cols(a):
+            return slice(a * P, (a + 1) * P)
+
+        def half_cols(h):
+            return slice(h * NODES // 2, (h + 1) * NODES // 2)
+
+        w_grp = const.tile([P, ORDERS, OUTS, PACK], BF16, align_bytes=64)
+        w_codes = const.tile([P, ORDERS * OUTS], U32, align_bytes=64)
+        w_scales = const.tile([P, ORDERS * OUTS], U8, align_bytes=64)
+        bias_sum = const.tile([P, OUTS], F32)
+        bias_col = const.tile([P, 1], F32)
+
+        def prepare_weights():
+            for k in range(ORDERS):
+                nc.vector.tensor_copy(
+                    out=w_grp[:, k],
+                    in_=w_nat[:, k, :].rearrange("p (t o) -> p o t", t=PACK),
+                )
+            for k in range(ORDERS):
+                nc.vector.quantize_mx(
+                    out=w_codes[:, tile_cols(k)].bitcast(FP8X4),
+                    scales=w_scales[:, tile_cols(k)],
+                    in_=w_grp[:, k].rearrange("p o t -> p (o t)"),
+                )
+            nc.vector.tensor_tensor(
+                out=bias_sum[:], in0=b_all[:, tile_cols(0)], in1=b_all[:, tile_cols(1)], op=ALU.add
+            )
+            nc.vector.tensor_tensor(
+                out=bias_sum[:], in0=bias_sum[:], in1=b_all[:, tile_cols(2)], op=ALU.add
+            )
+            bank = turned.tile([P, P], F32, tag="turned")
+            nc.tensor.transpose(bank[:], bias_sum[:], ident[:])
+            nc.vector.tensor_copy(out=bias_col[:], in_=bank[:, 0:1])
+
+        def degrees(g):
+            deg_t = small.tile([P, TILES], F32, tag="deg")
+            for a in range(TILES):
+                nc.scalar.activation(
+                    out=scrap[:, a, :], in_=adj_nat[g][:, a, :], func=ACT.Copy,
+                    accum_out=deg_t[:, a : a + 1],
+                )
+            deg[g] = deg_t
+
+        def roots(g):
+            root_t = small.tile([P, TILES], F32, tag="root")
+            nc.scalar.activation(out=root_t[:], in_=deg[g][:], func=ACT.Sqrt, bias=eps[:, 0:1])
+            root[g] = root_t
+
+        def inverse_roots(g):
+            inv_t = small.tile([P, TILES], F32, tag="inv")
+            nc.vector.reciprocal(out=inv_t[:], in_=root[g][:])
+            inv[g] = inv_t
+
+        def scale_rows(g):
+            rows_t = work.tile([P, TILES, NODES], F32, tag="rows")
+            for a in range(TILES):
+                nc.vector.tensor_scalar(
+                    out=rows_t[:, a, :].rearrange("p (t m) -> p t m", t=PACK),
+                    in0=adj_nat[g][:, a, :].rearrange("p (m t) -> p t m", t=PACK),
+                    scalar1=inv[g][:, a : a + 1], scalar2=-1.0, op0=ALU.mult, op1=ALU.mult,
+                )
+            rows[g] = rows_t
+
+        def add_diagonal(g):
+            for a in range(TILES):
+                block = rows[g][:, a, tile_cols(a)]
+                nc.vector.scalar_tensor_tensor(
+                    out=block, in0=ident[:], scalar=root[g][:, a : a + 1], in1=block,
+                    op0=ALU.mult, op1=ALU.add,
+                )
+
+        def turn_rows(g, a):
+            bank = chain.tile([P, PACK, P], F32, tag="chain")
+            for t in range(PACK):
+                nc.tensor.transpose(bank[:, t, :], rows[g][:, a, tile_cols(t)], ident[:])
+            rows_turned[g, a] = bank
+
+        def laplacian(g):
+            lap_t = work.tile([P, NODES, PACK], BF16, tag="lap_grp", align_bytes=64)
+            for a in range(TILES):
+                nc.vector.tensor_tensor(
+                    out=lap_t[:, tile_cols(a), :],
+                    in0=rows_turned[g, a][:].rearrange("p t c -> p c t"),
+                    in1=inv[g][:].unsqueeze(1).to_broadcast([P, P, PACK]),
+                    op=ALU.mult,
+                )
+            lap_grp[g] = lap_t
+
+        def group_by_node(g):
+            grp = work.tile([P, FEATS, PACK], BF16, tag="tx1_node_grp", align_bytes=64)
+            src = tx1_nat[g][:].rearrange("p t (m v) -> p v m t", v=PACK)
+            dst = grp[:].rearrange("p (v m) t -> p v m t", v=PACK)
+            for h in range(2):
+                nc.scalar.copy(out=dst[:, 2 * h : 2 * h + 2], in_=src[:, 2 * h : 2 * h + 2])
+            tx1_node_grp[g] = grp
+
+        def turn_features(nat, tag):
+            grp = work.tile([P, NODES, PACK], BF16, tag=tag, name=tag, align_bytes=64)
+            words_in = nat[:].bitcast(F32)
+            words_out = (
+                grp[:].rearrange("p i t -> p (i t)").bitcast(F32).rearrange("p (i u) -> p i u", u=2)
+            )
+            for h in range(2):
+                bank = turned.tile([P, 2, 2 * P], F32, tag="turned")
+                for u in range(2):
+                    for a2 in range(2):
+                        nc.tensor.transpose(
+                            bank[:, u, tile_cols(a2)], words_in[:, 2 * h + a2, u : 2 * P : 2], ident[:]
+                        )
+                nc.scalar.copy(
+                    out=words_out[:, 2 * P * h : 2 * P * (h + 1), :],
+                    in_=bank[:].rearrange("p u c -> p c u"),
+                )
+            return grp
+
+        def first_product(g):
+            for a in range(TILES):
+                bank = chain.tile([P, PACK, P], F32, tag="chain")
+                for v in range(PACK):
+                    mx(bank[:, v, :], tx1_node_q[g], tile_cols(v), lap_q[g], tile_cols(a), True, True)
+                prod[g, a] = bank
+
+        def second_order(g, a):
+            nc.vector.scalar_tensor_tensor(
+                out=tx2_grp[g][:, tile_cols(a), :],
+                in0=prod[g, a][:].rearrange("p v c -> p c v"),
+                scalar=2.0,
+                in1=x_grp[g][:, tile_cols(a), :],
+                op0=ALU.mult,
+                op1=ALU.subtract,
+            )
+
+        def output_product(g, h):
+            if h == 0:
+                out_by_feat[g] = work.tile([P, NODES], F32, tag="out_by_feat", name="out_by_feat")
+            acc = turned.tile([P, NODES // 2], F32, tag="turned")
+            terms = (x_q[g], tx1_feat_q[g], tx2_q[g])
+            for k in range(ORDERS):
+                mx(acc[:], (w_codes, w_scales), tile_cols(k), terms[k], half_cols(h),
+                   k == 0, k == ORDERS - 1)
+            nc.scalar.activation(
+                out=out_by_feat[g][:, half_cols(h)], in_=acc[:], func=ACT.Relu, bias=bias_col[:, 0:1]
+            )
+
+        def turn_output(g, h):
+            bank = turned.tile([P, 2, OUTS], F32, tag="turned")
+            for a2 in range(2):
+                nc.tensor.transpose(bank[:, a2, :], out_by_feat[g][:, tile_cols(2 * h + a2)], ident[:])
+            out_turned[g, h] = bank
+
+        def store_output(g, h):
+            if h == 0:
+                out_by_node[g] = work.tile([P, TILES, OUTS], F32, tag="out_by_node", name="out_by_node")
+            tiles = slice(2 * h, 2 * h + 2)
+            nc.scalar.copy(out=out_by_node[g][:, tiles, :], in_=out_turned[g, h][:])
+            nc.sync.dma_start(
+                out=out[g].rearrange("(p a) o -> p a o", p=P)[:, tiles, :], in_=out_by_node[g][:, tiles, :]
+            )
+
+        def live(g):
+            return 0 <= g < GRAPHS
+
+        for s in range(-2, GRAPHS + 1):
+            if s == -1:
+                prepare_weights()
+            if live(s - 1):
+                output_product(s - 1, 0)
+                output_product(s - 1, 1)
+            if live(s):
+                laplacian(s)
+            if live(s + 1):
+                x_grp[s + 1] = turn_features(x_nat[s + 1], "x_grp")
+            if live(s):
+                x_q[s] = quantise(x_grp[s], "x")
+            if live(s + 1):
+                inverse_roots(s + 1)
+            if live(s):
+                lap_q[s] = quantise(lap_grp[s], "lap")
+                first_product(s)
+            if live(s - 1):
+                turn_output(s - 1, 0)
+                turn_output(s - 1, 1)
+            if live(s + 1):
+                tx1_feat_grp[s + 1] = turn_features(tx1_nat[s + 1], "tx1_feat_grp")
+            if live(s - 1):
+                store_output(s - 1, 0)
+                store_output(s - 1, 1)
+            if live(s + 2):
+                degrees(s + 2)
+                roots(s + 2)
+                group_by_node(s + 2)
+            if live(s):
+                tx1_feat_q[s] = quantise(tx1_feat_grp[s], "tx1_feat")
+                tx2_grp[s] = work.tile([P, NODES, PACK], BF16, tag="tx2_grp", name="tx2_grp", align_bytes=64)
+                tx2_q[s] = mx_operand("tx2")
+            if live(s + 1):
+                scale_rows(s + 1)
+                add_diagonal(s + 1)
+            for a in range(TILES):
+                if live(s):
+                    second_order(s, a)
+                if live(s + 1):
+                    turn_rows(s + 1, a)
+                if live(s) and a == TILES - 2:
+                    quantise_cols(tx2_grp[s], tx2_q[s], half_cols(0))
+            if live(s + 1):
+                tx1_node_q[s + 1] = quantise(tx1_node_grp[s + 1], "tx1_node")
+            if live(s):
+                quantise_cols(tx2_grp[s], tx2_q[s], half_cols(1))

@@ -31,26 +31,31 @@ def tile_cheblayer_pb_kernel(tc, x, tx1, adj, W, b, out):
         inputs = ctx.enter_context(tc.tile_pool(name="inputs", bufs=GRAPHS))
         small = ctx.enter_context(tc.tile_pool(name="small", bufs=3))
         work = ctx.enter_context(tc.tile_pool(name="work", bufs=2))
-        chain = ctx.enter_context(tc.psum_pool(name="chain", bufs=TILES))
-        turned = ctx.enter_context(tc.psum_pool(name="turned", bufs=4))
+        deep = ctx.enter_context(tc.tile_pool(name="deep", bufs=3))
+        single = ctx.enter_context(tc.tile_pool(name="single", bufs=1))
+        prod_pool = ctx.enter_context(tc.psum_pool(name="prod_pool", bufs=TILES))
+        r_pool = ctx.enter_context(tc.psum_pool(name="r_pool", bufs=1))
+        turned = ctx.enter_context(tc.psum_pool(name="turned", bufs=3))
         ctx.enter_context(tc.manual_schedule())
 
         x_nat, tx1_nat, adj_nat = {}, {}, {}
-        deg, root, inv, rows = {}, {}, {}, {}
-        x_grp, lap_q, tx1_node_q, x_q, tx1_feat_q, tx2_q = {}, {}, {}, {}, {}, {}
-        tx1_feat_grp, tx1_node_grp, lap_grp, tx2_grp = {}, {}, {}, {}
-        rows_turned, prod, out_by_feat, out_turned, out_by_node = {}, {}, {}, {}, {}
+        neg_adj, neg_deg, root, inv, degree, r_cols, lap = {}, {}, {}, {}, {}, {}, {}
+        x_grp, tx1_feat_grp, tx1_node_grp, lap_grp, tx2_grp = {}, {}, {}, {}, {}
+        lap_q, tx1_node_q, x_q, tx1_feat_q, tx2_q = {}, {}, {}, {}, {}
+        prod, out_by_feat, out_turned, out_by_node = {}, {}, {}, {}
 
         eps = const.tile([P, 1], F32)
-        nc.vector.memset(eps[:], EPS)
+        nc.vector.memset(eps[:], 0.0)
+        nc.vector.tensor_scalar(out=eps[:], in0=eps[:], scalar1=EPS, scalar2=None, op0=ALU.add)
         warm = const.tile([P, 1], F32)
         nc.scalar.activation(out=warm[:], in_=eps[:], func=ACT.Sqrt)
         ident = const.tile([P, P], F32)
         make_identity(nc, ident[:])
-        scrap = const.tile([P, TILES, NODES], BF16)
+        b_rows = const.tile([P, OUTS], BF16)
+        nc.vector.memset(b_rows[:], 0.0)
 
         def load_adjacency(g, pieces):
-            adj_t = inputs.tile([P, TILES, NODES], BF16, tag="adj_nat")
+            adj_t = inputs.tile([P, TILES, NODES], BF16, tag="adj_nat", name="adj_nat")
             adj_rows = adj[g].rearrange("(p a) j -> p a j", p=P)
             step = TILES // pieces
             for a in range(0, TILES, step):
@@ -58,18 +63,17 @@ def tile_cheblayer_pb_kernel(tc, x, tx1, adj, W, b, out):
             adj_nat[g] = adj_t
 
         def load_features(g):
-            tx1_t = inputs.tile([P, TILES, FEATS], BF16, tag="tx1_nat")
+            tx1_t = inputs.tile([P, TILES, FEATS], BF16, tag="tx1_nat", name="tx1_nat")
             nc.sync.dma_start(out=tx1_t[:], in_=tx1[g].rearrange("(p a) f -> p a f", p=P))
-            x_t = inputs.tile([P, TILES, FEATS], BF16, tag="x_nat")
+            x_t = inputs.tile([P, TILES, FEATS], BF16, tag="x_nat", name="x_nat")
             nc.sync.dma_start(out=x_t[:], in_=x[g].rearrange("(p a) f -> p a f", p=P))
             tx1_nat[g], x_nat[g] = tx1_t, x_t
 
         load_adjacency(0, pieces=TILES)
+        load_features(0)
         w_nat = const.tile([P, ORDERS, PACK * OUTS], BF16)
         nc.sync.dma_start(out=w_nat[:], in_=W.rearrange("k (p t) o -> p k (t o)", t=PACK))
-        b_all = const.tile([P, ORDERS * OUTS], BF16)
-        nc.sync.dma_start(out=b_all[:], in_=b.rearrange("k o -> (k o)").partition_broadcast(P))
-        load_features(0)
+        nc.sync.dma_start(out=b_rows[0:ORDERS, :], in_=b)
         for g in range(1, GRAPHS):
             load_adjacency(g, pieces=1)
             load_features(g)
@@ -111,14 +115,13 @@ def tile_cheblayer_pb_kernel(tc, x, tx1, adj, W, b, out):
         w_grp = const.tile([P, ORDERS, OUTS, PACK], BF16, align_bytes=64)
         w_codes = const.tile([P, ORDERS * OUTS], U32, align_bytes=64)
         w_scales = const.tile([P, ORDERS * OUTS], U8, align_bytes=64)
-        bias_sum = const.tile([P, OUTS], F32)
+        b_wide = const.tile([P, OUTS], F32)
         bias_col = const.tile([P, 1], F32)
 
         def prepare_weights():
             for k in range(ORDERS):
                 nc.vector.tensor_copy(
-                    out=w_grp[:, k],
-                    in_=w_nat[:, k, :].rearrange("p (t o) -> p o t", t=PACK),
+                    out=w_grp[:, k], in_=w_nat[:, k, :].rearrange("p (t o) -> p o t", t=PACK)
                 )
             for k in range(ORDERS):
                 nc.vector.quantize_mx(
@@ -126,100 +129,102 @@ def tile_cheblayer_pb_kernel(tc, x, tx1, adj, W, b, out):
                     scales=w_scales[:, tile_cols(k)],
                     in_=w_grp[:, k].rearrange("p o t -> p (o t)"),
                 )
-            nc.vector.tensor_tensor(
-                out=bias_sum[:], in0=b_all[:, tile_cols(0)], in1=b_all[:, tile_cols(1)], op=ALU.add
-            )
-            nc.vector.tensor_tensor(
-                out=bias_sum[:], in0=bias_sum[:], in1=b_all[:, tile_cols(2)], op=ALU.add
-            )
-            bank = turned.tile([P, P], F32, tag="turned")
-            nc.tensor.transpose(bank[:], bias_sum[:], ident[:])
-            nc.vector.tensor_copy(out=bias_col[:], in_=bank[:, 0:1])
+            nc.vector.tensor_copy(out=b_wide[:], in_=b_rows[:])
+            bank = turned.tile([P, P], F32, tag="turned", name="turned_b")
+            nc.tensor.transpose(bank[:], b_wide[:], ident[:])
+            nc.vector.reduce_sum(out=bias_col[:], in_=bank[:, 0:ORDERS], axis=mybir.AxisListType.X)
 
-        def degrees(g):
-            deg_t = small.tile([P, TILES], F32, tag="deg")
-            for a in range(TILES):
+        def negate_adjacency(g, tiles):
+            if 0 in tiles:
+                neg_adj[g] = work.tile([P, TILES, NODES], F32, tag="neg_adj", name="neg_adj")
+                neg_deg[g] = small.tile([P, TILES], F32, tag="neg_deg", name="neg_deg")
+            for a in tiles:
                 nc.scalar.activation(
-                    out=scrap[:, a, :], in_=adj_nat[g][:, a, :], func=ACT.Copy,
-                    accum_out=deg_t[:, a : a + 1],
+                    out=neg_adj[g][:, a, :].rearrange("p (t m) -> p t m", t=PACK),
+                    in_=adj_nat[g][:, a, :].rearrange("p (m t) -> p t m", t=PACK),
+                    func=ACT.Copy, scale=-1.0, accum_out=neg_deg[g][:, a : a + 1],
                 )
-            deg[g] = deg_t
 
         def roots(g):
-            root_t = small.tile([P, TILES], F32, tag="root")
-            nc.scalar.activation(out=root_t[:], in_=deg[g][:], func=ACT.Sqrt, bias=eps[:, 0:1])
+            root_t = small.tile([P, TILES], F32, tag="root", name="root")
+            nc.scalar.activation(
+                out=root_t[:], in_=neg_deg[g][:], func=ACT.Sqrt, scale=-1.0, bias=eps[:, 0:1]
+            )
             root[g] = root_t
 
         def inverse_roots(g):
-            inv_t = small.tile([P, TILES], F32, tag="inv")
+            degree_t = small.tile([P, TILES], F32, tag="degree", name="degree")
+            nc.gpsimd.tensor_tensor(out=degree_t[:], in0=root[g][:], in1=root[g][:], op=ALU.mult)
+            degree[g] = degree_t
+            inv_t = small.tile([P, TILES], F32, tag="inv", name="inv")
             nc.vector.reciprocal(out=inv_t[:], in_=root[g][:])
             inv[g] = inv_t
-
-        def scale_rows(g):
-            rows_t = work.tile([P, TILES, NODES], F32, tag="rows")
-            for a in range(TILES):
-                nc.vector.tensor_scalar(
-                    out=rows_t[:, a, :].rearrange("p (t m) -> p t m", t=PACK),
-                    in0=adj_nat[g][:, a, :].rearrange("p (m t) -> p t m", t=PACK),
-                    scalar1=inv[g][:, a : a + 1], scalar2=-1.0, op0=ALU.mult, op1=ALU.mult,
+            bank = r_pool.tile([P, NODES], F32, tag="r", name="r_bank")
+            for t in range(PACK):
+                nc.tensor.transpose(
+                    bank[:, tile_cols(t)], inv_t[:, t : t + 1].to_broadcast([P, P]), ident[:]
                 )
-            rows[g] = rows_t
+            r_cols[g] = bank
 
         def add_diagonal(g):
             for a in range(TILES):
-                block = rows[g][:, a, tile_cols(a)]
+                block = neg_adj[g][:, a, tile_cols(a)]
                 nc.vector.scalar_tensor_tensor(
-                    out=block, in0=ident[:], scalar=root[g][:, a : a + 1], in1=block,
+                    out=block, in0=ident[:], scalar=degree[g][:, a : a + 1], in1=block,
                     op0=ALU.mult, op1=ALU.add,
                 )
 
-        def turn_rows(g, a):
-            bank = chain.tile([P, PACK, P], F32, tag="chain")
-            for t in range(PACK):
-                nc.tensor.transpose(bank[:, t, :], rows[g][:, a, tile_cols(t)], ident[:])
-            rows_turned[g, a] = bank
-
-        def laplacian(g):
-            lap_t = work.tile([P, NODES, PACK], BF16, tag="lap_grp", align_bytes=64)
-            for a in range(TILES):
-                nc.vector.tensor_tensor(
-                    out=lap_t[:, tile_cols(a), :],
-                    in0=rows_turned[g, a][:].rearrange("p t c -> p c t"),
-                    in1=inv[g][:].unsqueeze(1).to_broadcast([P, P, PACK]),
-                    op=ALU.mult,
+        def laplacian(g, a):
+            if a == 0:
+                lap[g] = work.tile([P, TILES, NODES], BF16, tag="lap", name="lap")
+            for u in range(2):
+                nc.vector.scalar_tensor_tensor(
+                    out=lap[g][:, a, half_cols(u)].rearrange("p (m e) -> p m e", e=2),
+                    in0=neg_adj[g][:, a, half_cols(u)].rearrange("p (e m) -> p m e", e=2),
+                    scalar=inv[g][:, a : a + 1],
+                    in1=r_cols[g][:, half_cols(u)].rearrange("p (e m) -> p m e", e=2),
+                    op0=ALU.mult, op1=ALU.mult,
                 )
-            lap_grp[g] = lap_t
 
         def group_by_node(g):
-            grp = work.tile([P, FEATS, PACK], BF16, tag="tx1_node_grp", align_bytes=64)
+            grp = single.tile([P, FEATS, PACK], BF16, tag="tx1_node_grp", name="tx1_node_grp", align_bytes=64)
             src = tx1_nat[g][:].rearrange("p t (m v) -> p v m t", v=PACK)
             dst = grp[:].rearrange("p (v m) t -> p v m t", v=PACK)
-            for h in range(2):
-                nc.scalar.copy(out=dst[:, 2 * h : 2 * h + 2], in_=src[:, 2 * h : 2 * h + 2])
+            for v in range(PACK):
+                if g == 0:
+                    nc.vector.tensor_copy(out=dst[:, v], in_=src[:, v])
+                else:
+                    nc.gpsimd.tensor_scalar(
+                        out=dst[:, v], in0=src[:, v], scalar1=1.0, scalar2=0.0, op0=ALU.mult, op1=ALU.add
+                    )
             tx1_node_grp[g] = grp
 
-        def turn_features(nat, tag):
-            grp = work.tile([P, NODES, PACK], BF16, tag=tag, name=tag, align_bytes=64)
-            words_in = nat[:].bitcast(F32)
+        def turn_words(h, words, grp):
             words_out = (
                 grp[:].rearrange("p i t -> p (i t)").bitcast(F32).rearrange("p (i u) -> p i u", u=2)
             )
+            bank = turned.tile([P, 2, 2 * P], F32, tag="turned", name="turned_w")
+            for u in range(2):
+                for a2 in range(2):
+                    nc.tensor.transpose(bank[:, u, tile_cols(a2)], words(2 * h + a2, u), ident[:])
+            nc.scalar.copy(out=words_out[:, half_cols(h), :], in_=bank[:].rearrange("p u c -> p c u"))
+
+        def turn_features(nat, tag):
+            grp = deep.tile([P, NODES, PACK], BF16, tag=tag, name=tag, align_bytes=64)
+            rows = nat[:].bitcast(F32)
             for h in range(2):
-                bank = turned.tile([P, 2, 2 * P], F32, tag="turned")
-                for u in range(2):
-                    for a2 in range(2):
-                        nc.tensor.transpose(
-                            bank[:, u, tile_cols(a2)], words_in[:, 2 * h + a2, u : 2 * P : 2], ident[:]
-                        )
-                nc.scalar.copy(
-                    out=words_out[:, 2 * P * h : 2 * P * (h + 1), :],
-                    in_=bank[:].rearrange("p u c -> p c u"),
-                )
+                turn_words(h, lambda a, u: rows[:, a, u : 2 * P : 2], grp)
             return grp
+
+        def turn_laplacian(g, h):
+            if h == 0:
+                lap_grp[g] = work.tile([P, NODES, PACK], BF16, tag="lap_grp", name="lap_grp", align_bytes=64)
+            rows = lap[g][:].bitcast(F32)
+            turn_words(h, lambda a, u: rows[:, a, tile_cols(u)], lap_grp[g])
 
         def first_product(g):
             for a in range(TILES):
-                bank = chain.tile([P, PACK, P], F32, tag="chain")
+                bank = prod_pool.tile([P, PACK, P], F32, tag="prod", name="prod")
                 for v in range(PACK):
                     mx(bank[:, v, :], tx1_node_q[g], tile_cols(v), lap_q[g], tile_cols(a), True, True)
                 prod[g, a] = bank
@@ -237,7 +242,7 @@ def tile_cheblayer_pb_kernel(tc, x, tx1, adj, W, b, out):
         def output_product(g, h):
             if h == 0:
                 out_by_feat[g] = work.tile([P, NODES], F32, tag="out_by_feat", name="out_by_feat")
-            acc = turned.tile([P, NODES // 2], F32, tag="turned")
+            acc = turned.tile([P, NODES // 2], F32, tag="turned", name="turned_acc")
             terms = (x_q[g], tx1_feat_q[g], tx2_q[g])
             for k in range(ORDERS):
                 mx(acc[:], (w_codes, w_scales), tile_cols(k), terms[k], half_cols(h),
@@ -247,7 +252,7 @@ def tile_cheblayer_pb_kernel(tc, x, tx1, adj, W, b, out):
             )
 
         def turn_output(g, h):
-            bank = turned.tile([P, 2, OUTS], F32, tag="turned")
+            bank = turned.tile([P, 2, OUTS], F32, tag="turned", name="turned_out")
             for a2 in range(2):
                 nc.tensor.transpose(bank[:, a2, :], out_by_feat[g][:, tile_cols(2 * h + a2)], ident[:])
             out_turned[g, h] = bank
@@ -265,49 +270,48 @@ def tile_cheblayer_pb_kernel(tc, x, tx1, adj, W, b, out):
             return 0 <= g < GRAPHS
 
         for s in range(-2, GRAPHS + 1):
-            if s == -1:
-                prepare_weights()
+            if live(s):
+                lap_q[s] = quantise(lap_grp[s], "lap")
             if live(s - 1):
                 output_product(s - 1, 0)
                 output_product(s - 1, 1)
             if live(s):
-                laplacian(s)
-            if live(s + 1):
-                x_grp[s + 1] = turn_features(x_nat[s + 1], "x_grp")
-            if live(s):
-                x_q[s] = quantise(x_grp[s], "x")
-            if live(s + 1):
-                inverse_roots(s + 1)
-            if live(s):
-                lap_q[s] = quantise(lap_grp[s], "lap")
                 first_product(s)
-            if live(s - 1):
-                turn_output(s - 1, 0)
-                turn_output(s - 1, 1)
-            if live(s + 1):
-                tx1_feat_grp[s + 1] = turn_features(tx1_nat[s + 1], "tx1_feat_grp")
-            if live(s - 1):
-                store_output(s - 1, 0)
-                store_output(s - 1, 1)
             if live(s + 2):
-                degrees(s + 2)
+                negate_adjacency(s + 2, range(TILES))
                 roots(s + 2)
-                group_by_node(s + 2)
-            if live(s):
-                tx1_feat_q[s] = quantise(tx1_feat_grp[s], "tx1_feat")
-                tx2_grp[s] = work.tile([P, NODES, PACK], BF16, tag="tx2_grp", name="tx2_grp", align_bytes=64)
-                tx2_q[s] = mx_operand("tx2")
-            if live(s + 1):
-                scale_rows(s + 1)
-                add_diagonal(s + 1)
-            for a in range(TILES):
-                if live(s):
-                    second_order(s, a)
-                if live(s + 1):
-                    turn_rows(s + 1, a)
-                if live(s) and a == TILES - 2:
-                    quantise_cols(tx2_grp[s], tx2_q[s], half_cols(0))
+                tx1_feat_grp[s + 2] = turn_features(tx1_nat[s + 2], "tx1_feat_grp")
             if live(s + 1):
                 tx1_node_q[s + 1] = quantise(tx1_node_grp[s + 1], "tx1_node")
+                add_diagonal(s + 1)
+            if live(s + 2):
+                group_by_node(s + 2)
+            if live(s + 1):
+                for a in range(TILES):
+                    laplacian(s + 1, a)
+            if live(s - 1):
+                for h in range(2):
+                    turn_output(s - 1, h)
+                for h in range(2):
+                    store_output(s - 1, h)
+            if live(s + 1):
+                turn_laplacian(s + 1, 0)
+                turn_laplacian(s + 1, 1)
+            if live(s + 2):
+                x_grp[s + 2] = turn_features(x_nat[s + 2], "x_grp")
+            if s == -1:
+                prepare_weights()
+            if live(s):
+                tx2_grp[s] = work.tile([P, NODES, PACK], BF16, tag="tx2_grp", name="tx2_grp", align_bytes=64)
+                tx2_q[s] = mx_operand("tx2")
+                for a in range(TILES):
+                    second_order(s, a)
+                    if a == TILES - 2:
+                        quantise_cols(tx2_grp[s], tx2_q[s], half_cols(0))
+            if live(s + 1):
+                x_q[s + 1] = quantise(x_grp[s + 1], "x")
+                tx1_feat_q[s + 1] = quantise(tx1_feat_grp[s + 1], "tx1_feat")
             if live(s):
                 quantise_cols(tx2_grp[s], tx2_q[s], half_cols(1))
+            if live(s + 2):
+                inverse_roots(s + 2)

@@ -51,12 +51,17 @@ def tile_cheblayer_pb_kernel(tc, x, tx1, adj, W, b, out):
         nc.scalar.activation(out=warm[:], in_=eps[:], func=ACT.Sqrt)
         ident = const.tile([P, P], F32)
         make_identity(nc, ident[:])
+        perm = const.tile([P, 2, P // 2], F32)
+        nc.vector.tensor_copy(
+            out=perm[:].rearrange("p u (m e) -> p u m e", e=2),
+            in_=ident[:].rearrange("p (m u e) -> p u m e", u=2, e=2),
+        )
         b_rows = const.tile([P, OUTS], BF16)
         nc.vector.memset(b_rows[:], 0.0)
 
         def load_adjacency(g, pieces):
             adj_t = inputs.tile([P, TILES, NODES], BF16, tag="adj_nat", name="adj_nat")
-            adj_rows = adj[g].rearrange("(p a) j -> p a j", p=P)
+            adj_rows = adj[g].rearrange("(a p) j -> p a j", p=P)
             step = TILES // pieces
             for a in range(0, TILES, step):
                 nc.sync.dma_start(out=adj_t[:, a : a + step, :], in_=adj_rows[:, a : a + step, :])
@@ -79,8 +84,8 @@ def tile_cheblayer_pb_kernel(tc, x, tx1, adj, W, b, out):
             load_features(g)
 
         def mx_operand(tag):
-            codes = work.tile([P, NODES], U32, tag=tag + "_codes", name=tag + "_codes", align_bytes=64)
-            scales = work.tile([P, NODES], U8, tag=tag + "_scales", name=tag + "_scales", align_bytes=64)
+            codes = deep.tile([P, NODES], U32, tag=tag + "_codes", name=tag + "_codes", align_bytes=64)
+            scales = deep.tile([P, NODES], U8, tag=tag + "_scales", name=tag + "_scales", align_bytes=64)
             return codes, scales
 
         def quantise_cols(grouped, operand, cols):
@@ -112,38 +117,53 @@ def tile_cheblayer_pb_kernel(tc, x, tx1, adj, W, b, out):
         def half_cols(h):
             return slice(h * NODES // 2, (h + 1) * NODES // 2)
 
+        def own_cols(row, a):
+            return row.rearrange("p (u b c) -> p u b c", u=2, b=TILES)[:, :, a, :]
+
         w_grp = const.tile([P, ORDERS, OUTS, PACK], BF16, align_bytes=64)
         w_codes = const.tile([P, ORDERS * OUTS], U32, align_bytes=64)
         w_scales = const.tile([P, ORDERS * OUTS], U8, align_bytes=64)
         b_wide = const.tile([P, OUTS], F32)
         bias_col = const.tile([P, 1], F32)
 
-        def prepare_weights():
+        def group_weights():
             for k in range(ORDERS):
-                nc.vector.tensor_copy(
-                    out=w_grp[:, k], in_=w_nat[:, k, :].rearrange("p (t o) -> p o t", t=PACK)
+                nc.gpsimd.tensor_scalar(
+                    out=w_grp[:, k], in0=w_nat[:, k, :].rearrange("p (t o) -> p o t", t=PACK),
+                    scalar1=1.0, scalar2=0.0, op0=ALU.mult, op1=ALU.add,
                 )
+
+        def quantise_weights():
             for k in range(ORDERS):
                 nc.vector.quantize_mx(
                     out=w_codes[:, tile_cols(k)].bitcast(FP8X4),
                     scales=w_scales[:, tile_cols(k)],
                     in_=w_grp[:, k].rearrange("p o t -> p (o t)"),
                 )
+
+        def turn_biases():
             nc.vector.tensor_copy(out=b_wide[:], in_=b_rows[:])
             bank = turned.tile([P, P], F32, tag="turned", name="turned_b")
             nc.tensor.transpose(bank[:], b_wide[:], ident[:])
+            return bank
+
+        def sum_biases(bank):
             nc.vector.reduce_sum(out=bias_col[:], in_=bank[:, 0:ORDERS], axis=mybir.AxisListType.X)
 
-        def negate_adjacency(g, tiles):
-            if 0 in tiles:
-                neg_adj[g] = work.tile([P, TILES, NODES], F32, tag="neg_adj", name="neg_adj")
-                neg_deg[g] = small.tile([P, TILES], F32, tag="neg_deg", name="neg_deg")
-            for a in tiles:
-                nc.scalar.activation(
-                    out=neg_adj[g][:, a, :].rearrange("p (t m) -> p t m", t=PACK),
-                    in_=adj_nat[g][:, a, :].rearrange("p (m t) -> p t m", t=PACK),
-                    func=ACT.Copy, scale=-1.0, accum_out=neg_deg[g][:, a : a + 1],
-                )
+        def negate_adjacency(g):
+            neg_adj[g] = work.tile([P, TILES, NODES], F32, tag="neg_adj", name="neg_adj")
+            neg_deg[g] = small.tile([P, TILES], F32, tag="neg_deg", name="neg_deg")
+            for a in range(TILES):
+                dst = neg_adj[g][:, a, :].rearrange("p (u m e) -> p u m e", u=2, e=2)
+                src = adj_nat[g][:, a, :].rearrange("p (m u e) -> p u m e", u=2, e=2)
+                row_sum = neg_deg[g][:, a : a + 1]
+                if g == 0 and a >= TILES // 2:
+                    nc.vector.tensor_scalar(
+                        out=dst, in0=src, scalar1=-1.0, scalar2=None, op0=ALU.mult, op1=ALU.add,
+                        accum_out=row_sum,
+                    )
+                else:
+                    nc.scalar.activation(out=dst, in_=src, func=ACT.Copy, scale=-1.0, accum_out=row_sum)
 
         def roots(g):
             root_t = small.tile([P, TILES], F32, tag="root", name="root")
@@ -160,31 +180,27 @@ def tile_cheblayer_pb_kernel(tc, x, tx1, adj, W, b, out):
             nc.vector.reciprocal(out=inv_t[:], in_=root[g][:])
             inv[g] = inv_t
             bank = r_pool.tile([P, NODES], F32, tag="r", name="r_bank")
-            for t in range(PACK):
+            for a in range(TILES):
                 nc.tensor.transpose(
-                    bank[:, tile_cols(t)], inv_t[:, t : t + 1].to_broadcast([P, P]), ident[:]
+                    own_cols(bank[:], a), inv_t[:, a : a + 1].to_broadcast([P, P]), perm[:]
                 )
             r_cols[g] = bank
 
         def add_diagonal(g):
             for a in range(TILES):
-                block = neg_adj[g][:, a, tile_cols(a)]
+                block = own_cols(neg_adj[g][:, a, :], a)
                 nc.vector.scalar_tensor_tensor(
-                    out=block, in0=ident[:], scalar=degree[g][:, a : a + 1], in1=block,
+                    out=block, in0=perm[:], scalar=degree[g][:, a : a + 1], in1=block,
                     op0=ALU.mult, op1=ALU.add,
                 )
 
         def laplacian(g, a):
             if a == 0:
                 lap[g] = work.tile([P, TILES, NODES], BF16, tag="lap", name="lap")
-            for u in range(2):
-                nc.vector.scalar_tensor_tensor(
-                    out=lap[g][:, a, half_cols(u)].rearrange("p (m e) -> p m e", e=2),
-                    in0=neg_adj[g][:, a, half_cols(u)].rearrange("p (e m) -> p m e", e=2),
-                    scalar=inv[g][:, a : a + 1],
-                    in1=r_cols[g][:, half_cols(u)].rearrange("p (e m) -> p m e", e=2),
-                    op0=ALU.mult, op1=ALU.mult,
-                )
+            nc.vector.scalar_tensor_tensor(
+                out=lap[g][:, a, :], in0=neg_adj[g][:, a, :], scalar=inv[g][:, a : a + 1],
+                in1=r_cols[g][:], op0=ALU.mult, op1=ALU.mult,
+            )
 
         def group_by_node(g):
             grp = single.tile([P, FEATS, PACK], BF16, tag="tx1_node_grp", name="tx1_node_grp", align_bytes=64)
@@ -199,35 +215,40 @@ def tile_cheblayer_pb_kernel(tc, x, tx1, adj, W, b, out):
                     )
             tx1_node_grp[g] = grp
 
-        def turn_words(h, words, grp):
-            words_out = (
-                grp[:].rearrange("p i t -> p (i t)").bitcast(F32).rearrange("p (i u) -> p i u", u=2)
-            )
-            bank = turned.tile([P, 2, 2 * P], F32, tag="turned", name="turned_w")
+        def turn_words(h, words):
+            bank = turned.tile([P, 2, 2, P], F32, tag="turned", name="turned_w")
             for u in range(2):
                 for a2 in range(2):
-                    nc.tensor.transpose(bank[:, u, tile_cols(a2)], words(2 * h + a2, u), ident[:])
-            nc.scalar.copy(out=words_out[:, half_cols(h), :], in_=bank[:].rearrange("p u c -> p c u"))
+                    nc.tensor.transpose(bank[:, u, a2, :], words(2 * h + a2, u), ident[:])
+            return bank
 
-        def turn_features(nat, tag):
-            grp = deep.tile([P, NODES, PACK], BF16, tag=tag, name=tag, align_bytes=64)
-            rows = nat[:].bitcast(F32)
-            for h in range(2):
-                turn_words(h, lambda a, u: rows[:, a, u : 2 * P : 2], grp)
-            return grp
+        def as_words(grp):
+            return grp[:].rearrange("p i t -> p (i t)").bitcast(F32).rearrange("p (i u) -> p i u", u=2)
+
+        def turn_features(nat, grp, tag, g, h):
+            if h == 0:
+                grp[g] = deep.tile([P, NODES, PACK], BF16, tag=tag, name=tag, align_bytes=64)
+            rows = nat[g][:].bitcast(F32)
+            bank = turn_words(h, lambda a, u: rows[:, a, u : 2 * P : 2])
+            nc.scalar.copy(
+                out=as_words(grp[g]).rearrange("p (n a) u -> p n a u", a=TILES)[:, :, 2 * h : 2 * h + 2, :],
+                in_=bank[:].rearrange("p u a n -> p n a u"),
+            )
 
         def turn_laplacian(g, h):
             if h == 0:
                 lap_grp[g] = work.tile([P, NODES, PACK], BF16, tag="lap_grp", name="lap_grp", align_bytes=64)
             rows = lap[g][:].bitcast(F32)
-            turn_words(h, lambda a, u: rows[:, a, tile_cols(u)], lap_grp[g])
+            bank = turn_words(h, lambda a, u: rows[:, a, tile_cols(u)])
+            nc.scalar.copy(
+                out=as_words(lap_grp[g])[:, half_cols(h), :], in_=bank[:].rearrange("p u a n -> p (a n) u")
+            )
 
-        def first_product(g):
-            for a in range(TILES):
-                bank = prod_pool.tile([P, PACK, P], F32, tag="prod", name="prod")
-                for v in range(PACK):
-                    mx(bank[:, v, :], tx1_node_q[g], tile_cols(v), lap_q[g], tile_cols(a), True, True)
-                prod[g, a] = bank
+        def first_product(g, a):
+            bank = prod_pool.tile([P, PACK, P], F32, tag="prod", name="prod")
+            for v in range(PACK):
+                mx(bank[:, v, :], tx1_node_q[g], tile_cols(v), lap_q[g], tile_cols(a), True, True)
+            prod[g, a] = bank
 
         def second_order(g, a):
             nc.vector.scalar_tensor_tensor(
@@ -239,79 +260,116 @@ def tile_cheblayer_pb_kernel(tc, x, tx1, adj, W, b, out):
                 op1=ALU.subtract,
             )
 
-        def output_product(g, h):
-            if h == 0:
+        def output_product(g, piece):
+            cols = slice(piece[0] * P, piece[1] * P)
+            if piece[0] == 0:
                 out_by_feat[g] = work.tile([P, NODES], F32, tag="out_by_feat", name="out_by_feat")
-            acc = turned.tile([P, NODES // 2], F32, tag="turned", name="turned_acc")
+            acc = turned.tile([P, cols.stop - cols.start], F32, tag="turned", name="turned_acc")
             terms = (x_q[g], tx1_feat_q[g], tx2_q[g])
             for k in range(ORDERS):
-                mx(acc[:], (w_codes, w_scales), tile_cols(k), terms[k], half_cols(h),
-                   k == 0, k == ORDERS - 1)
-            nc.scalar.activation(
-                out=out_by_feat[g][:, half_cols(h)], in_=acc[:], func=ACT.Relu, bias=bias_col[:, 0:1]
-            )
+                mx(acc[:], (w_codes, w_scales), tile_cols(k), terms[k], cols, k == 0, k == ORDERS - 1)
+            if by_vector(g, piece):
+                nc.vector.tensor_scalar(
+                    out=out_by_feat[g][:, cols], in0=acc[:], scalar1=bias_col[:, 0:1], scalar2=0.0,
+                    op0=ALU.add, op1=ALU.max,
+                )
+            else:
+                nc.scalar.activation(
+                    out=out_by_feat[g][:, cols], in_=acc[:], func=ACT.Relu, bias=bias_col[:, 0:1]
+                )
 
-        def turn_output(g, h):
-            bank = turned.tile([P, 2, OUTS], F32, tag="turned", name="turned_out")
-            for a2 in range(2):
-                nc.tensor.transpose(bank[:, a2, :], out_by_feat[g][:, tile_cols(2 * h + a2)], ident[:])
-            out_turned[g, h] = bank
+        def turn_output(g, piece):
+            bank = turned.tile([P, piece[1] - piece[0], OUTS], F32, tag="turned", name="turned_out")
+            for a in range(piece[0], piece[1]):
+                nc.tensor.transpose(bank[:, a - piece[0], :], out_by_feat[g][:, tile_cols(a)], ident[:])
+            out_turned[g, piece] = bank
 
-        def store_output(g, h):
-            if h == 0:
+        def store_output(g, piece):
+            if piece[0] == 0:
                 out_by_node[g] = work.tile([P, TILES, OUTS], F32, tag="out_by_node", name="out_by_node")
-            tiles = slice(2 * h, 2 * h + 2)
-            nc.scalar.copy(out=out_by_node[g][:, tiles, :], in_=out_turned[g, h][:])
+            tiles = slice(piece[0], piece[1])
+            copy = nc.vector.tensor_copy if by_vector(g, piece) else nc.scalar.copy
+            copy(out=out_by_node[g][:, tiles, :], in_=out_turned[g, piece][:])
             nc.sync.dma_start(
-                out=out[g].rearrange("(p a) o -> p a o", p=P)[:, tiles, :], in_=out_by_node[g][:, tiles, :]
+                out=out[g].rearrange("(a p) o -> p a o", p=P)[:, tiles, :], in_=out_by_node[g][:, tiles, :]
             )
 
         def live(g):
             return 0 <= g < GRAPHS
 
+        last = GRAPHS - 1
+        halves = ((0, 2), (2, 4))
+        pieces = {g: halves if g < last else ((0, 2), (2, 3), (3, 4)) for g in range(GRAPHS)}
+
+        def by_vector(g, piece):
+            return g == last and piece == pieces[last][1]
+
+        def quantise_tx2(g, piece):
+            quantise_cols(tx2_grp[g], tx2_q[g], slice(piece[0] * P, piece[1] * P))
+
         for s in range(-2, GRAPHS + 1):
             if live(s):
-                lap_q[s] = quantise(lap_grp[s], "lap")
-            if live(s - 1):
-                output_product(s - 1, 0)
-                output_product(s - 1, 1)
-            if live(s):
-                first_product(s)
+                lap_q[s] = mx_operand("lap")
+                for h in range(2) if s == last else (0,):
+                    quantise_cols(lap_grp[s], lap_q[s], half_cols(h) if s == last else slice(0, NODES))
+                    for a in range(2 * h, 2 * h + 2) if s == last else range(TILES):
+                        first_product(s, a)
+            if s == 0:
+                sum_biases(b_bank)
+            if live(s - 1) and s - 1 < last:
+                quantise_tx2(s - 1, (0, TILES))
+            if s == -1:
+                group_weights()
+                add_diagonal(0)
+                for a in range(TILES):
+                    laplacian(0, a)
+                turn_laplacian(0, 0)
+                turn_laplacian(0, 1)
+                group_by_node(0)
             if live(s + 2):
-                negate_adjacency(s + 2, range(TILES))
+                negate_adjacency(s + 2)
                 roots(s + 2)
-                tx1_feat_grp[s + 2] = turn_features(tx1_nat[s + 2], "tx1_feat_grp")
-            if live(s + 1):
-                tx1_node_q[s + 1] = quantise(tx1_node_grp[s + 1], "tx1_node")
-                add_diagonal(s + 1)
+            if live(s - 1):
+                for piece in pieces[s - 1]:
+                    output_product(s - 1, piece)
             if live(s + 2):
-                group_by_node(s + 2)
+                turn_features(tx1_nat, tx1_feat_grp, "tx1_feat_grp", s + 2, 0)
+                if s + 2 == 0:
+                    inverse_roots(0)
+                turn_features(tx1_nat, tx1_feat_grp, "tx1_feat_grp", s + 2, 1)
             if live(s + 1):
+                tx1_feat_q[s + 1] = quantise(tx1_feat_grp[s + 1], "tx1_feat")
+                x_q[s + 1] = quantise(x_grp[s + 1], "x")
+                tx1_node_q[s + 1] = quantise(tx1_node_grp[s + 1], "tx1_node")
+            if s >= 0 and live(s + 1):
+                add_diagonal(s + 1)
+            if s >= -1 and live(s + 2):
+                group_by_node(s + 2)
+            if s >= 0 and live(s + 1):
                 for a in range(TILES):
                     laplacian(s + 1, a)
             if live(s - 1):
-                for h in range(2):
-                    turn_output(s - 1, h)
-                for h in range(2):
-                    store_output(s - 1, h)
-            if live(s + 1):
+                for piece in pieces[s - 1]:
+                    turn_output(s - 1, piece)
+                    store_output(s - 1, piece)
+            if s >= 0 and live(s + 1):
                 turn_laplacian(s + 1, 0)
                 turn_laplacian(s + 1, 1)
             if live(s + 2):
-                x_grp[s + 2] = turn_features(x_nat[s + 2], "x_grp")
+                turn_features(x_nat, x_grp, "x_grp", s + 2, 0)
+                turn_features(x_nat, x_grp, "x_grp", s + 2, 1)
             if s == -1:
-                prepare_weights()
+                quantise_weights()
+                b_bank = turn_biases()
             if live(s):
                 tx2_grp[s] = work.tile([P, NODES, PACK], BF16, tag="tx2_grp", name="tx2_grp", align_bytes=64)
                 tx2_q[s] = mx_operand("tx2")
                 for a in range(TILES):
                     second_order(s, a)
-                    if a == TILES - 2:
-                        quantise_cols(tx2_grp[s], tx2_q[s], half_cols(0))
-            if live(s + 1):
-                x_q[s + 1] = quantise(x_grp[s + 1], "x")
-                tx1_feat_q[s + 1] = quantise(tx1_feat_grp[s + 1], "tx1_feat")
-            if live(s):
-                quantise_cols(tx2_grp[s], tx2_q[s], half_cols(1))
-            if live(s + 2):
+                    if s == last and a == TILES - 2:
+                        quantise_tx2(s, halves[0])
+                if s == last:
+                    quantise_tx2(s, (2, 3))
+                    quantise_tx2(s, (3, 4))
+            if s >= -1 and live(s + 2):
                 inverse_roots(s + 2)

@@ -42,7 +42,7 @@ def tile_cheblayer_pb_kernel(tc, x, tx1, adj, W, b, out):
         neg_adj, neg_deg, root, inv, degree, r_cols, lap = {}, {}, {}, {}, {}, {}, {}
         x_grp, tx1_feat_grp, tx1_node_grp, lap_grp, tx2_grp = {}, {}, {}, {}, {}
         lap_q, tx1_node_q, x_q, tx1_feat_q, tx2_q = {}, {}, {}, {}, {}
-        prod, out_by_feat, out_turned, out_by_node = {}, {}, {}, {}
+        prod, out_acc, out_by_feat, out_turned, out_by_node = {}, {}, {}, {}, {}
 
         eps = const.tile([P, 1], F32)
         nc.vector.memset(eps[:], 0.0)
@@ -204,14 +204,16 @@ def tile_cheblayer_pb_kernel(tc, x, tx1, adj, W, b, out):
 
         def group_by_node(g):
             grp = single.tile([P, FEATS, PACK], BF16, tag="tx1_node_grp", name="tx1_node_grp", align_bytes=64)
-            src = tx1_nat[g][:].rearrange("p t (m v) -> p v m t", v=PACK)
-            dst = grp[:].rearrange("p (v m) t -> p v m t", v=PACK)
-            for v in range(PACK):
+            src = tx1_nat[g][:].rearrange("p t (m v) -> p m t v", v=PACK)
+            dst = grp[:].rearrange("p (v m) t -> p m t v", v=PACK)
+            for c in range(PACK):
+                part = slice(c * P // PACK, (c + 1) * P // PACK)
                 if g == 0:
-                    nc.vector.tensor_copy(out=dst[:, v], in_=src[:, v])
+                    nc.vector.tensor_copy(out=dst[:, part], in_=src[:, part])
                 else:
                     nc.gpsimd.tensor_scalar(
-                        out=dst[:, v], in0=src[:, v], scalar1=1.0, scalar2=0.0, op0=ALU.mult, op1=ALU.add
+                        out=dst[:, part], in0=src[:, part], scalar1=1.0, scalar2=0.0,
+                        op0=ALU.mult, op1=ALU.add,
                     )
             tx1_node_grp[g] = grp
 
@@ -268,6 +270,11 @@ def tile_cheblayer_pb_kernel(tc, x, tx1, adj, W, b, out):
             terms = (x_q[g], tx1_feat_q[g], tx2_q[g])
             for k in range(ORDERS):
                 mx(acc[:], (w_codes, w_scales), tile_cols(k), terms[k], cols, k == 0, k == ORDERS - 1)
+            out_acc[g, piece] = acc
+
+        def output_relu(g, piece):
+            acc = out_acc[g, piece]
+            cols = slice(piece[0] * P, piece[1] * P)
             if by_vector(g, piece):
                 nc.vector.tensor_scalar(
                     out=out_by_feat[g][:, cols], in0=acc[:], scalar1=bias_col[:, 0:1], scalar2=0.0,
@@ -312,12 +319,11 @@ def tile_cheblayer_pb_kernel(tc, x, tx1, adj, W, b, out):
                 lap_q[s] = mx_operand("lap")
                 for h in range(2) if s == last else (0,):
                     quantise_cols(lap_grp[s], lap_q[s], half_cols(h) if s == last else slice(0, NODES))
-                    for a in range(2 * h, 2 * h + 2) if s == last else range(TILES):
-                        first_product(s, a)
             if s == 0:
                 sum_biases(b_bank)
-            if live(s - 1) and s - 1 < last:
-                quantise_tx2(s - 1, (0, TILES))
+            if live(s):
+                for a in range(TILES):
+                    first_product(s, a)
             if s == -1:
                 group_weights()
                 add_diagonal(0)
@@ -326,38 +332,46 @@ def tile_cheblayer_pb_kernel(tc, x, tx1, adj, W, b, out):
                 turn_laplacian(0, 0)
                 turn_laplacian(0, 1)
                 group_by_node(0)
+            if s >= 0 and live(s + 1):
+                add_diagonal(s + 1)
+            if live(s - 1) and s - 1 < last:
+                quantise_tx2(s - 1, (0, TILES))
             if live(s + 2):
                 negate_adjacency(s + 2)
                 roots(s + 2)
-            if live(s - 1):
-                for piece in pieces[s - 1]:
-                    output_product(s - 1, piece)
             if live(s + 2):
                 turn_features(tx1_nat, tx1_feat_grp, "tx1_feat_grp", s + 2, 0)
                 if s + 2 == 0:
                     inverse_roots(0)
+            if live(s + 2):
                 turn_features(tx1_nat, tx1_feat_grp, "tx1_feat_grp", s + 2, 1)
             if live(s + 1):
                 tx1_feat_q[s + 1] = quantise(tx1_feat_grp[s + 1], "tx1_feat")
                 x_q[s + 1] = quantise(x_grp[s + 1], "x")
                 tx1_node_q[s + 1] = quantise(tx1_node_grp[s + 1], "tx1_node")
-            if s >= 0 and live(s + 1):
-                add_diagonal(s + 1)
             if s >= -1 and live(s + 2):
                 group_by_node(s + 2)
             if s >= 0 and live(s + 1):
                 for a in range(TILES):
                     laplacian(s + 1, a)
+            if s >= 0 and live(s + 1):
+                turn_laplacian(s + 1, 0)
+            if s >= 0 and live(s + 1):
+                turn_laplacian(s + 1, 1)
+            if live(s + 2):
+                turn_features(x_nat, x_grp, "x_grp", s + 2, 0)
+            if live(s + 2):
+                turn_features(x_nat, x_grp, "x_grp", s + 2, 1)
+            if live(s - 1):
+                for piece in pieces[s - 1]:
+                    output_product(s - 1, piece)
+            if live(s - 1):
+                for piece in pieces[s - 1]:
+                    output_relu(s - 1, piece)
             if live(s - 1):
                 for piece in pieces[s - 1]:
                     turn_output(s - 1, piece)
                     store_output(s - 1, piece)
-            if s >= 0 and live(s + 1):
-                turn_laplacian(s + 1, 0)
-                turn_laplacian(s + 1, 1)
-            if live(s + 2):
-                turn_features(x_nat, x_grp, "x_grp", s + 2, 0)
-                turn_features(x_nat, x_grp, "x_grp", s + 2, 1)
             if s == -1:
                 quantise_weights()
                 b_bank = turn_biases()

@@ -40,7 +40,7 @@ def tile_cheblayer_pb_kernel(tc, x, tx1, adj, W, b, out):
 
         x_nat, tx1_nat, adj_nat = {}, {}, {}
         neg_adj, neg_deg, root, inv, degree, r_cols, lap = {}, {}, {}, {}, {}, {}, {}
-        x_grp, tx1_feat_grp, tx1_node_grp, lap_grp, tx2_grp = {}, {}, {}, {}, {}
+        x_grp, tx1_feat_grp, tx1_node_grp, lap_grp, tx2_grp, feat_grp, feat_q = {}, {}, {}, {}, {}, {}, {}
         lap_q, tx1_node_q, x_q, tx1_feat_q, tx2_q = {}, {}, {}, {}, {}
         prod, out_acc, out_by_feat, out_turned, out_by_node = {}, {}, {}, {}, {}
 
@@ -52,10 +52,6 @@ def tile_cheblayer_pb_kernel(tc, x, tx1, adj, W, b, out):
         ident = const.tile([P, P], F32)
         make_identity(nc, ident[:])
         perm = const.tile([P, 2, P // 2], F32)
-        nc.vector.tensor_copy(
-            out=perm[:].rearrange("p u (m e) -> p u m e", e=2),
-            in_=ident[:].rearrange("p (m u e) -> p u m e", u=2, e=2),
-        )
         b_rows = const.tile([P, OUTS], BF16)
         nc.vector.memset(b_rows[:], 0.0)
 
@@ -95,6 +91,13 @@ def tile_cheblayer_pb_kernel(tc, x, tx1, adj, W, b, out):
                 in_=grouped[:, cols, :].rearrange("p c t -> p (c t)"),
             )
 
+        def quantise_features(g):
+            codes = deep.tile([P, 2 * NODES], U32, tag="feat_codes", name="feat_codes", align_bytes=64)
+            scales = deep.tile([P, 2 * NODES], U8, tag="feat_scales", name="feat_scales", align_bytes=64)
+            quantise_cols(feat_grp[g], (codes, scales), slice(0, 2 * NODES))
+            x_q[g] = codes[:, 0:NODES], scales[:, 0:NODES]
+            tx1_feat_q[g] = codes[:, NODES : 2 * NODES], scales[:, NODES : 2 * NODES]
+
         def quantise(grouped, tag):
             operand = mx_operand(tag)
             quantise_cols(grouped, operand, slice(0, NODES))
@@ -119,6 +122,12 @@ def tile_cheblayer_pb_kernel(tc, x, tx1, adj, W, b, out):
 
         def own_cols(row, a):
             return row.rearrange("p (u b c) -> p u b c", u=2, b=TILES)[:, :, a, :]
+
+        def permute_identity():
+            nc.vector.tensor_copy(
+                out=perm[:].rearrange("p u (m e) -> p u m e", e=2),
+                in_=ident[:].rearrange("p (m u e) -> p u m e", u=2, e=2),
+            )
 
         w_grp = const.tile([P, ORDERS, OUTS, PACK], BF16, align_bytes=64)
         w_codes = const.tile([P, ORDERS * OUTS], U32, align_bytes=64)
@@ -204,8 +213,8 @@ def tile_cheblayer_pb_kernel(tc, x, tx1, adj, W, b, out):
 
         def group_by_node(g):
             grp = single.tile([P, FEATS, PACK], BF16, tag="tx1_node_grp", name="tx1_node_grp", align_bytes=64)
-            src = tx1_nat[g][:].rearrange("p t (m v) -> p m t v", v=PACK)
-            dst = grp[:].rearrange("p (v m) t -> p m t v", v=PACK)
+            src = tx1_nat[g][:].rearrange("p t (m v) -> p m v t", v=PACK)
+            dst = grp[:].rearrange("p (v m) t -> p m v t", v=PACK)
             for c in range(PACK):
                 part = slice(c * P // PACK, (c + 1) * P // PACK)
                 if g == 0:
@@ -228,8 +237,10 @@ def tile_cheblayer_pb_kernel(tc, x, tx1, adj, W, b, out):
             return grp[:].rearrange("p i t -> p (i t)").bitcast(F32).rearrange("p (i u) -> p i u", u=2)
 
         def turn_features(nat, grp, tag, g, h):
-            if h == 0:
-                grp[g] = deep.tile([P, NODES, PACK], BF16, tag=tag, name=tag, align_bytes=64)
+            if tag == "tx1_feat_grp" and h == 0:
+                feat_grp[g] = deep.tile([P, 2 * NODES, PACK], BF16, tag="feat_grp", name="feat_grp", align_bytes=64)
+            part = feat_grp[g][:, 0:NODES, :] if tag == "x_grp" else feat_grp[g][:, NODES : 2 * NODES, :]
+            grp[g] = part
             rows = nat[g][:].bitcast(F32)
             bank = turn_words(h, lambda a, u: rows[:, a, u : 2 * P : 2])
             nc.scalar.copy(
@@ -339,6 +350,8 @@ def tile_cheblayer_pb_kernel(tc, x, tx1, adj, W, b, out):
             if live(s + 2):
                 negate_adjacency(s + 2)
                 roots(s + 2)
+            if s == -2:
+                permute_identity()
             if live(s + 2):
                 turn_features(tx1_nat, tx1_feat_grp, "tx1_feat_grp", s + 2, 0)
                 if s + 2 == 0:
@@ -346,8 +359,7 @@ def tile_cheblayer_pb_kernel(tc, x, tx1, adj, W, b, out):
             if live(s + 2):
                 turn_features(tx1_nat, tx1_feat_grp, "tx1_feat_grp", s + 2, 1)
             if live(s + 1):
-                tx1_feat_q[s + 1] = quantise(tx1_feat_grp[s + 1], "tx1_feat")
-                x_q[s + 1] = quantise(x_grp[s + 1], "x")
+                quantise_features(s + 1)
                 tx1_node_q[s + 1] = quantise(tx1_node_grp[s + 1], "tx1_node")
             if s >= -1 and live(s + 2):
                 group_by_node(s + 2)

@@ -52,6 +52,8 @@ def tile_cheblayer_pb_kernel(tc, x, tx1, adj, W, b, out):
         ident = const.tile([P, P], F32)
         make_identity(nc, ident[:])
         perm = const.tile([P, 2, P // 2], F32)
+        zeros = const.tile([P, NODES], BF16)
+        nc.vector.memset(zeros[:], 0.0)
         b_rows = const.tile([P, OUTS], BF16)
         nc.vector.memset(b_rows[:], 0.0)
 
@@ -136,11 +138,9 @@ def tile_cheblayer_pb_kernel(tc, x, tx1, adj, W, b, out):
         bias_col = const.tile([P, 1], F32)
 
         def group_weights():
-            for k in range(ORDERS):
-                nc.gpsimd.tensor_scalar(
-                    out=w_grp[:, k], in0=w_nat[:, k, :].rearrange("p (t o) -> p o t", t=PACK),
-                    scalar1=1.0, scalar2=0.0, op0=ALU.mult, op1=ALU.add,
-                )
+            nc.vector.tensor_copy(
+                out=w_grp[:], in_=w_nat[:].rearrange("p k (t o) -> p k o t", t=PACK)
+            )
 
         def quantise_weights():
             for k in range(ORDERS):
@@ -215,19 +215,21 @@ def tile_cheblayer_pb_kernel(tc, x, tx1, adj, W, b, out):
             grp = single.tile([P, FEATS, PACK], BF16, tag="tx1_node_grp", name="tx1_node_grp", align_bytes=64)
             src = tx1_nat[g][:].rearrange("p t (m v) -> p m v t", v=PACK)
             dst = grp[:].rearrange("p (v m) t -> p m v t", v=PACK)
-            for c in range(PACK):
-                part = slice(c * P // PACK, (c + 1) * P // PACK)
-                if g == 0:
-                    nc.vector.tensor_copy(out=dst[:, part], in_=src[:, part])
-                else:
-                    nc.gpsimd.tensor_scalar(
-                        out=dst[:, part], in0=src[:, part], scalar1=1.0, scalar2=0.0,
-                        op0=ALU.mult, op1=ALU.add,
-                    )
+            if g < 2:
+                nc.vector.tensor_copy(out=dst, in_=src)
+            else:
+                nc.gpsimd.tensor_scalar(
+                    out=dst, in0=src, scalar1=1.0, scalar2=0.0, op0=ALU.mult, op1=ALU.add
+                )
             tx1_node_grp[g] = grp
 
-        def turn_words(h, words):
+        def turn_words(h, words, busy=False):
             bank = turned.tile([P, 2, 2, P], F32, tag="turned", name="turned_w")
+            if busy:
+                nc.tensor.matmul(
+                    bank[:].rearrange("p u a n -> p (u a n)"), lhsT=zeros[:, 0:P], rhs=zeros[:],
+                    start=True, stop=True,
+                )
             for u in range(2):
                 for a2 in range(2):
                     nc.tensor.transpose(bank[:, u, a2, :], words(2 * h + a2, u), ident[:])
@@ -242,7 +244,7 @@ def tile_cheblayer_pb_kernel(tc, x, tx1, adj, W, b, out):
             part = feat_grp[g][:, 0:NODES, :] if tag == "x_grp" else feat_grp[g][:, NODES : 2 * NODES, :]
             grp[g] = part
             rows = nat[g][:].bitcast(F32)
-            bank = turn_words(h, lambda a, u: rows[:, a, u : 2 * P : 2])
+            bank = turn_words(h, lambda a, u: rows[:, a, u : 2 * P : 2], (tag[0], h) in ())
             nc.scalar.copy(
                 out=as_words(grp[g]).rearrange("p (n a) u -> p n a u", a=TILES)[:, :, 2 * h : 2 * h + 2, :],
                 in_=bank[:].rearrange("p u a n -> p n a u"),
@@ -252,7 +254,7 @@ def tile_cheblayer_pb_kernel(tc, x, tx1, adj, W, b, out):
             if h == 0:
                 lap_grp[g] = work.tile([P, NODES, PACK], BF16, tag="lap_grp", name="lap_grp", align_bytes=64)
             rows = lap[g][:].bitcast(F32)
-            bank = turn_words(h, lambda a, u: rows[:, a, tile_cols(u)])
+            bank = turn_words(h, lambda a, u: rows[:, a, tile_cols(u)], h in (0,1))
             nc.scalar.copy(
                 out=as_words(lap_grp[g])[:, half_cols(h), :], in_=bank[:].rearrange("p u a n -> p (a n) u")
             )
@@ -336,7 +338,6 @@ def tile_cheblayer_pb_kernel(tc, x, tx1, adj, W, b, out):
                 for a in range(TILES):
                     first_product(s, a)
             if s == -1:
-                group_weights()
                 add_diagonal(0)
                 for a in range(TILES):
                     laplacian(0, a)
@@ -354,8 +355,8 @@ def tile_cheblayer_pb_kernel(tc, x, tx1, adj, W, b, out):
                 permute_identity()
             if live(s + 2):
                 turn_features(tx1_nat, tx1_feat_grp, "tx1_feat_grp", s + 2, 0)
-                if s + 2 == 0:
-                    inverse_roots(0)
+            if s == -2:
+                inverse_roots(0)
             if live(s + 2):
                 turn_features(tx1_nat, tx1_feat_grp, "tx1_feat_grp", s + 2, 1)
             if live(s + 1):
@@ -385,6 +386,7 @@ def tile_cheblayer_pb_kernel(tc, x, tx1, adj, W, b, out):
                     turn_output(s - 1, piece)
                     store_output(s - 1, piece)
             if s == -1:
+                group_weights()
                 quantise_weights()
                 b_bank = turn_biases()
             if live(s):

@@ -318,8 +318,8 @@ def tile_cheblayer_pb_kernel(tc, x, tx1, adj, W, b, out):
             return 0 <= g < GRAPHS
 
         last = GRAPHS - 1
-        halves = ((0, 2), (2, 4))
-        pieces = {g: halves if g < last else ((0, 2), (2, 3), (3, 4)) for g in range(GRAPHS)}
+        pieces = {g: ((0, TILES),) if g < last - 3 else ((0, 2), (2, 4)) for g in range(last)}
+        pieces[last] = ((0, 2), (2, 3), (3, 4))
 
         def by_vector(g, piece):
             return g == last and piece == pieces[last][1]
@@ -335,7 +335,7 @@ def tile_cheblayer_pb_kernel(tc, x, tx1, adj, W, b, out):
             if s == 0:
                 sum_biases(b_bank)
             if live(s):
-                for a in range(TILES):
+                for a in (0, 1,):
                     first_product(s, a)
             if s == -1:
                 add_diagonal(0)
@@ -350,13 +350,23 @@ def tile_cheblayer_pb_kernel(tc, x, tx1, adj, W, b, out):
                 quantise_tx2(s - 1, (0, TILES))
             if live(s + 2):
                 negate_adjacency(s + 2)
-                roots(s + 2)
             if s == -2:
                 permute_identity()
+            if s == -2:
+                roots(0)
             if live(s + 2):
                 turn_features(tx1_nat, tx1_feat_grp, "tx1_feat_grp", s + 2, 0)
+            if s > -2 and live(s + 2):
+                roots(s + 2)
             if s == -2:
                 inverse_roots(0)
+            if live(s):
+                for a in (2, 3,):
+                    first_product(s, a)
+            if live(s - 2) and s - 2 < last - 3:
+                for piece in pieces[s - 2]:
+                    turn_output(s - 2, piece)
+                    store_output(s - 2, piece)
             if live(s + 2):
                 turn_features(tx1_nat, tx1_feat_grp, "tx1_feat_grp", s + 2, 1)
             if live(s + 1):
@@ -381,7 +391,7 @@ def tile_cheblayer_pb_kernel(tc, x, tx1, adj, W, b, out):
             if live(s - 1):
                 for piece in pieces[s - 1]:
                     output_relu(s - 1, piece)
-            if live(s - 1):
+            if live(s - 1) and s - 1 >= last - 3:
                 for piece in pieces[s - 1]:
                     turn_output(s - 1, piece)
                     store_output(s - 1, piece)
@@ -395,9 +405,9 @@ def tile_cheblayer_pb_kernel(tc, x, tx1, adj, W, b, out):
                 for a in range(TILES):
                     second_order(s, a)
                     if s == last and a == TILES - 2:
-                        quantise_tx2(s, halves[0])
+                        quantise_tx2(s, pieces[s][0])
                 if s == last:
-                    quantise_tx2(s, (2, 3))
-                    quantise_tx2(s, (3, 4))
+                    quantise_tx2(s, pieces[s][1])
+                    quantise_tx2(s, pieces[s][2])
             if s >= -1 and live(s + 2):
                 inverse_roots(s + 2)

from contextlib import ExitStack

import concourse.mybir as mybir
from concourse.masks import make_identity

F32 = mybir.dt.float32
BF16 = mybir.dt.bfloat16
U32 = mybir.dt.uint32
U8 = mybir.dt.uint8
FP8X4 = mybir.dt.float8_e4m3fn_x4
ALU = mybir.AluOpType
ACT = mybir.ActivationFunctionType

P = 128
PACK = 4
GRAPHS = 8
NODES = 512
FEATS = 512
OUTS = 128
ORDERS = 3
TILES = NODES // P
EPS = 1e-6

FLOPS = 2 * GRAPHS * (NODES * NODES * FEATS + ORDERS * NODES * FEATS * OUTS)


def tile_cheblayer_pb_kernel(tc, x, tx1, adj, W, b, out):
    nc = tc.nc
    with ExitStack() as ctx:
        const = ctx.enter_context(tc.tile_pool(name="const", bufs=1))
        inputs = ctx.enter_context(tc.tile_pool(name="inputs", bufs=GRAPHS))
        small = ctx.enter_context(tc.tile_pool(name="small", bufs=3))
        work = ctx.enter_context(tc.tile_pool(name="work", bufs=2))
        deep = ctx.enter_context(tc.tile_pool(name="deep", bufs=3))
        single = ctx.enter_context(tc.tile_pool(name="single", bufs=1))
        prod_pool = ctx.enter_context(tc.psum_pool(name="prod_pool", bufs=TILES))
        r_pool = ctx.enter_context(tc.psum_pool(name="r_pool", bufs=1))
        turned = ctx.enter_context(tc.psum_pool(name="turned", bufs=3))
        ctx.enter_context(tc.manual_schedule())

        x_nat, tx1_nat, adj_nat = {}, {}, {}
        neg_adj, neg_deg, root, inv, degree, r_cols, lap = {}, {}, {}, {}, {}, {}, {}
        x_grp, tx1_feat_grp, tx1_node_grp, lap_grp, tx2_grp, feat_grp, feat_q = {}, {}, {}, {}, {}, {}, {}
        lap_q, tx1_node_q, x_q, tx1_feat_q, tx2_q = {}, {}, {}, {}, {}
        prod, out_acc, out_by_feat, out_turned, out_by_node = {}, {}, {}, {}, {}

        eps = const.tile([P, 1], F32)
        nc.vector.memset(eps[:], 0.0)
        nc.vector.tensor_scalar(out=eps[:], in0=eps[:], scalar1=EPS, scalar2=None, op0=ALU.add)
        warm = const.tile([P, 1], F32)
        nc.scalar.activation(out=warm[:], in_=eps[:], func=ACT.Sqrt)
        ident = const.tile([P, P], F32)
        make_identity(nc, ident[:])
        perm = const.tile([P, 2, P // 2], F32)
        zeros = const.tile([P, NODES], BF16)
        nc.vector.memset(zeros[:], 0.0)
        b_rows = const.tile([P, OUTS], BF16)
        nc.vector.memset(b_rows[:], 0.0)

        def load_adjacency(g, pieces):
            adj_t = inputs.tile([P, TILES, NODES], BF16, tag="adj_nat", name="adj_nat")
            adj_rows = adj[g].rearrange("(a p) j -> p a j", p=P)
            step = TILES // pieces
            for a in range(0, TILES, step):
                nc.sync.dma_start(out=adj_t[:, a : a + step, :], in_=adj_rows[:, a : a + step, :])
            adj_nat[g] = adj_t

        def load_features(g):
            tx1_t = inputs.tile([P, TILES, FEATS], BF16, tag="tx1_nat", name="tx1_nat")
            nc.sync.dma_start(out=tx1_t[:], in_=tx1[g].rearrange("(p a) f -> p a f", p=P))
            x_t = inputs.tile([P, TILES, FEATS], BF16, tag="x_nat", name="x_nat")
            nc.sync.dma_start(out=x_t[:], in_=x[g].rearrange("(p a) f -> p a f", p=P))
            tx1_nat[g], x_nat[g] = tx1_t, x_t

        load_adjacency(0, pieces=TILES)
        load_features(0)
        w_nat = const.tile([P, ORDERS, PACK * OUTS], BF16)
        nc.sync.dma_start(out=w_nat[:], in_=W.rearrange("k (p t) o -> p k (t o)", t=PACK))
        nc.sync.dma_start(out=b_rows[0:ORDERS, :], in_=b)
        for g in range(1, GRAPHS):
            load_adjacency(g, pieces=1)
            load_features(g)

        def mx_operand(tag):
            codes = deep.tile([P, NODES], U32, tag=tag + "_codes", name=tag + "_codes", align_bytes=64)
            scales = deep.tile([P, NODES], U8, tag=tag + "_scales", name=tag + "_scales", align_bytes=64)
            return codes, scales

        def quantise_cols(grouped, operand, cols):
            nc.vector.quantize_mx(
                out=operand[0][:, cols].bitcast(FP8X4),
                scales=operand[1][:, cols],
                in_=grouped[:, cols, :].rearrange("p c t -> p (c t)"),
            )

        def quantise_features(g):
            codes = deep.tile([P, 2 * NODES], U32, tag="feat_codes", name="feat_codes", align_bytes=64)
            scales = deep.tile([P, 2 * NODES], U8, tag="feat_scales", name="feat_scales", align_bytes=64)
            quantise_cols(feat_grp[g], (codes, scales), slice(0, 2 * NODES))
            x_q[g] = codes[:, 0:NODES], scales[:, 0:NODES]
            tx1_feat_q[g] = codes[:, NODES : 2 * NODES], scales[:, NODES : 2 * NODES]

        def quantise(grouped, tag):
            operand = mx_operand(tag)
            quantise_cols(grouped, operand, slice(0, NODES))
            return operand

        def mx(out_ap, stationary, s_cols, moving, m_cols, start, stop):
            nc.tensor.matmul_mx(
                out=out_ap,
                lhsT=stationary[0][:, s_cols].bitcast(FP8X4),
                lhsT_scale=stationary[1][:, s_cols],
                rhs=moving[0][:, m_cols].bitcast(FP8X4),
                rhs_scale=moving[1][:, m_cols],
                start=start,
                stop=stop,
            )

        def tile_cols(a):
            return slice(a * P, (a + 1) * P)

        def half_cols(h):
            return slice(h * NODES // 2, (h + 1) * NODES // 2)

        def own_cols(row, a):
            return row.rearrange("p (u b c) -> p u b c", u=2, b=TILES)[:, :, a, :]

        def permute_identity():
            nc.vector.tensor_copy(
                out=perm[:].rearrange("p u (m e) -> p u m e", e=2),
                in_=ident[:].rearrange("p (m u e) -> p u m e", u=2, e=2),
            )

        w_grp = const.tile([P, ORDERS, OUTS, PACK], BF16, align_bytes=64)
        w_codes = const.tile([P, ORDERS * OUTS], U32, align_bytes=64)
        w_scales = const.tile([P, ORDERS * OUTS], U8, align_bytes=64)
        b_wide = const.tile([P, OUTS], F32)
        bias_col = const.tile([P, 1], F32)

        def group_weights():
            nc.vector.tensor_copy(
                out=w_grp[:], in_=w_nat[:].rearrange("p k (t o) -> p k o t", t=PACK)
            )

        def quantise_weights():
            for k in range(ORDERS):
                nc.vector.quantize_mx(
                    out=w_codes[:, tile_cols(k)].bitcast(FP8X4),
                    scales=w_scales[:, tile_cols(k)],
                    in_=w_grp[:, k].rearrange("p o t -> p (o t)"),
                )

        def turn_biases():
            nc.vector.tensor_copy(out=b_wide[:], in_=b_rows[:])
            bank = turned.tile([P, P], F32, tag="turned", name="turned_b")
            nc.tensor.transpose(bank[:], b_wide[:], ident[:])
            return bank

        def sum_biases(bank):
            nc.vector.reduce_sum(out=bias_col[:], in_=bank[:, 0:ORDERS], axis=mybir.AxisListType.X)

        def negate_adjacency(g):
            neg_adj[g] = work.tile([P, TILES, NODES], F32, tag="neg_adj", name="neg_adj")
            neg_deg[g] = small.tile([P, TILES], F32, tag="neg_deg", name="neg_deg")
            for a in range(TILES):
                dst = neg_adj[g][:, a, :].rearrange("p (u m e) -> p u m e", u=2, e=2)
                src = adj_nat[g][:, a, :].rearrange("p (m u e) -> p u m e", u=2, e=2)
                row_sum = neg_deg[g][:, a : a + 1]
                if g == 0 and a >= TILES // 2:
                    nc.vector.tensor_scalar(
                        out=dst, in0=src, scalar1=-1.0, scalar2=None, op0=ALU.mult, op1=ALU.add,
                        accum_out=row_sum,
                    )
                else:
                    nc.scalar.activation(out=dst, in_=src, func=ACT.Copy, scale=-1.0, accum_out=row_sum)

        def roots(g):
            root_t = small.tile([P, TILES], F32, tag="root", name="root")
            nc.scalar.activation(
                out=root_t[:], in_=neg_deg[g][:], func=ACT.Sqrt, scale=-1.0, bias=eps[:, 0:1]
            )
            root[g] = root_t

        def inverse_roots(g):
            degree_t = small.tile([P, TILES], F32, tag="degree", name="degree")
            nc.gpsimd.tensor_tensor(out=degree_t[:], in0=root[g][:], in1=root[g][:], op=ALU.mult)
            degree[g] = degree_t
            inv_t = small.tile([P, TILES], F32, tag="inv", name="inv")
            nc.vector.reciprocal(out=inv_t[:], in_=root[g][:])
            inv[g] = inv_t
            bank = r_pool.tile([P, NODES], F32, tag="r", name="r_bank")
            for a in range(TILES):
                nc.tensor.transpose(
                    own_cols(bank[:], a), inv_t[:, a : a + 1].to_broadcast([P, P]), perm[:]
                )
            r_cols[g] = bank

        def add_diagonal(g):
            for a in range(TILES):
                block = own_cols(neg_adj[g][:, a, :], a)
                nc.vector.scalar_tensor_tensor(
                    out=block, in0=perm[:], scalar=degree[g][:, a : a + 1], in1=block,
                    op0=ALU.mult, op1=ALU.add,
                )

        def laplacian(g, a):
            if a == 0:
                lap[g] = work.tile([P, TILES, NODES], BF16, tag="lap", name="lap")
            nc.vector.scalar_tensor_tensor(
                out=lap[g][:, a, :], in0=neg_adj[g][:, a, :], scalar=inv[g][:, a : a + 1],
                in1=r_cols[g][:], op0=ALU.mult, op1=ALU.mult,
            )

        def group_by_node(g):
            grp = single.tile([P, FEATS, PACK], BF16, tag="tx1_node_grp", name="tx1_node_grp", align_bytes=64)
            src = tx1_nat[g][:].rearrange("p t (m v) -> p m v t", v=PACK)
            dst = grp[:].rearrange("p (v m) t -> p m v t", v=PACK)
            if g < 2:
                nc.vector.tensor_copy(out=dst, in_=src)
            else:
                nc.gpsimd.tensor_scalar(
                    out=dst, in0=src, scalar1=1.0, scalar2=0.0, op0=ALU.mult, op1=ALU.add
                )
            tx1_node_grp[g] = grp

        def turn_words(h, words, busy=False):
            bank = turned.tile([P, 2, 2, P], F32, tag="turned", name="turned_w")
            if busy:
                nc.tensor.matmul(
                    bank[:].rearrange("p u a n -> p (u a n)"), lhsT=zeros[:, 0:P], rhs=zeros[:],
                    start=True, stop=True,
                )
            for u in range(2):
                for a2 in range(2):
                    nc.tensor.transpose(bank[:, u, a2, :], words(2 * h + a2, u), ident[:])
            return bank

        def as_words(grp):
            return grp[:].rearrange("p i t -> p (i t)").bitcast(F32).rearrange("p (i u) -> p i u", u=2)

        def turn_features(nat, grp, tag, g, h):
            if tag == "tx1_feat_grp" and h == 0:
                feat_grp[g] = deep.tile([P, 2 * NODES, PACK], BF16, tag="feat_grp", name="feat_grp", align_bytes=64)
            part = feat_grp[g][:, 0:NODES, :] if tag == "x_grp" else feat_grp[g][:, NODES : 2 * NODES, :]
            grp[g] = part
            rows = nat[g][:].bitcast(F32)
            bank = turn_words(h, lambda a, u: rows[:, a, u : 2 * P : 2], (tag[0], h) in ())
            nc.scalar.copy(
                out=as_words(grp[g]).rearrange("p (n a) u -> p n a u", a=TILES)[:, :, 2 * h : 2 * h + 2, :],
                in_=bank[:].rearrange("p u a n -> p n a u"),
            )

        def turn_laplacian(g, h):
            if h == 0:
                lap_grp[g] = work.tile([P, NODES, PACK], BF16, tag="lap_grp", name="lap_grp", align_bytes=64)
            rows = lap[g][:].bitcast(F32)
            bank = turn_words(h, lambda a, u: rows[:, a, tile_cols(u)], h in (0,1))
            nc.scalar.copy(
                out=as_words(lap_grp[g])[:, half_cols(h), :], in_=bank[:].rearrange("p u a n -> p (a n) u")
            )

        def first_product(g, a):
            bank = prod_pool.tile([P, PACK, P], F32, tag="prod", name="prod")
            for v in range(PACK):
                mx(bank[:, v, :], tx1_node_q[g], tile_cols(v), lap_q[g], tile_cols(a), True, True)
            prod[g, a] = bank

        def second_order(g, a):
            nc.vector.scalar_tensor_tensor(
                out=tx2_grp[g][:, tile_cols(a), :],
                in0=prod[g, a][:].rearrange("p v c -> p c v"),
                scalar=2.0,
                in1=x_grp[g][:, tile_cols(a), :],
                op0=ALU.mult,
                op1=ALU.subtract,
            )

        def output_product(g, piece):
            cols = slice(piece[0] * P, piece[1] * P)
            if piece[0] == 0:
                out_by_feat[g] = work.tile([P, NODES], F32, tag="out_by_feat", name="out_by_feat")
            acc = turned.tile([P, cols.stop - cols.start], F32, tag="turned", name="turned_acc")
            terms = (x_q[g], tx1_feat_q[g], tx2_q[g])
            for k in range(ORDERS):
                mx(acc[:], (w_codes, w_scales), tile_cols(k), terms[k], cols, k == 0, k == ORDERS - 1)
            out_acc[g, piece] = acc

        def output_relu(g, piece):
            acc = out_acc[g, piece]
            cols = slice(piece[0] * P, piece[1] * P)
            if by_vector(g, piece):
                nc.vector.tensor_scalar(
                    out=out_by_feat[g][:, cols], in0=acc[:], scalar1=bias_col[:, 0:1], scalar2=0.0,
                    op0=ALU.add, op1=ALU.max,
                )
            else:
                nc.scalar.activation(
                    out=out_by_feat[g][:, cols], in_=acc[:], func=ACT.Relu, bias=bias_col[:, 0:1]
                )

        def turn_output(g, piece):
            bank = turned.tile([P, piece[1] - piece[0], OUTS], F32, tag="turned", name="turned_out")
            for a in range(piece[0], piece[1]):
                nc.tensor.transpose(bank[:, a - piece[0], :], out_by_feat[g][:, tile_cols(a)], ident[:])
            out_turned[g, piece] = bank

        def store_output(g, piece):
            if piece[0] == 0:
                out_by_node[g] = work.tile([P, TILES, OUTS], F32, tag="out_by_node", name="out_by_node")
            tiles = slice(piece[0], piece[1])
            copy = nc.vector.tensor_copy if by_vector(g, piece) else nc.scalar.copy
            copy(out=out_by_node[g][:, tiles, :], in_=out_turned[g, piece][:])
            nc.sync.dma_start(
                out=out[g].rearrange("(a p) o -> p a o", p=P)[:, tiles, :], in_=out_by_node[g][:, tiles, :]
            )

        def live(g):
            return 0 <= g < GRAPHS

        last = GRAPHS - 1
        pieces = {g: ((0, TILES),) if g < last - 3 else ((0, 2), (2, 4)) for g in range(last)}
        pieces[last] = ((0, 2), (2, 3), (3, 4))

        def by_vector(g, piece):
            return g == last and piece == pieces[last][1]

        def quantise_tx2(g, piece):
            quantise_cols(tx2_grp[g], tx2_q[g], slice(piece[0] * P, piece[1] * P))

        for s in range(-2, GRAPHS + 1):
            if live(s):
                lap_q[s] = mx_operand("lap")
                for h in range(2) if s == last else (0,):
                    quantise_cols(lap_grp[s], lap_q[s], half_cols(h) if s == last else slice(0, NODES))
            if s == 0:
                sum_biases(b_bank)
            if live(s):
                for a in (0, 1,):
                    first_product(s, a)
            if s == -1:
                add_diagonal(0)
                for a in range(TILES):
                    laplacian(0, a)
                turn_laplacian(0, 0)
                turn_laplacian(0, 1)
                group_by_node(0)
            if s >= 0 and live(s + 1):
                add_diagonal(s + 1)
            if live(s - 1) and s - 1 < last:
                quantise_tx2(s - 1, (0, TILES))
            if live(s + 2):
                negate_adjacency(s + 2)
            if s == -2:
                permute_identity()
            if s == -2:
                roots(0)
            if live(s + 2):
                turn_features(tx1_nat, tx1_feat_grp, "tx1_feat_grp", s + 2, 0)
            if s > -2 and live(s + 2):
                roots(s + 2)
            if s == -2:
                inverse_roots(0)
            if live(s):
                for a in (2, 3,):
                    first_product(s, a)
            if live(s - 2) and s - 2 < last - 3:
                for piece in pieces[s - 2]:
                    turn_output(s - 2, piece)
                    store_output(s - 2, piece)
            if live(s + 2):
                turn_features(tx1_nat, tx1_feat_grp, "tx1_feat_grp", s + 2, 1)
            if live(s + 1):
                quantise_features(s + 1)
                tx1_node_q[s + 1] = quantise(tx1_node_grp[s + 1], "tx1_node")
            if s >= -1 and live(s + 2):
                group_by_node(s + 2)
            if s >= 0 and live(s + 1):
                for a in range(TILES):
                    laplacian(s + 1, a)
            if s >= 0 and live(s + 1):
                turn_laplacian(s + 1, 0)
            if s >= 0 and live(s + 1):
                turn_laplacian(s + 1, 1)
            if live(s + 2):
                turn_features(x_nat, x_grp, "x_grp", s + 2, 0)
            if live(s + 2):
                turn_features(x_nat, x_grp, "x_grp", s + 2, 1)
            if live(s - 1):
                for piece in pieces[s - 1]:
                    output_product(s - 1, piece)
            if live(s - 1):
                for piece in pieces[s - 1]:
                    output_relu(s - 1, piece)
            if live(s - 1) and s - 1 >= last - 3:
                for piece in pieces[s - 1]:
                    turn_output(s - 1, piece)
                    store_output(s - 1, piece)
            if s == -1:
                group_weights()
                quantise_weights()
                b_bank = turn_biases()
            if live(s):
                tx2_grp[s] = work.tile([P, NODES, PACK], BF16, tag="tx2_grp", name="tx2_grp", align_bytes=64)
                tx2_q[s] = mx_operand("tx2")
                for a in range(TILES):
                    second_order(s, a)
                    if s == last and a == TILES - 2:
                        quantise_tx2(s, pieces[s][0])
                if s == last:
                    quantise_tx2(s, pieces[s][1])
                    quantise_tx2(s, pieces[s][2])
            if s >= -1 and live(s + 2):
                inverse_roots(s + 2)
